import numpy as np
import ml_dtypes

BF16 = ml_dtypes.bfloat16


def bf(x):
    return np.asarray(x, np.float32).astype(BF16)


def f32(x):
    return np.asarray(x, np.float32)


def f64(x):
    return np.asarray(x).astype(np.float64)


def striped(idx):
    return np.tile(idx.reshape(-1, 16).T, (8, 1))


S, D, K, M, H, N, R = 1024, 128, 4, 256, 2048, 4096, 512


def setup_inputs():
    return {"table": bf(np.random.standard_normal((S, D))), "w0_self": bf(np.random.standard_normal((D, M)) / np.sqrt(D)), "w0_nb": bf(np.random.standard_normal((D, M)) / np.sqrt(D)), "w1_self": bf(np.random.standard_normal((M, H)) / np.sqrt(M)), "w1_nb": bf(np.random.standard_normal((M, H)) / np.sqrt(M)), "offs": striped(np.concatenate([np.random.permutation(S)[:R] for _ in range(N // R)]))}


def reference(table, w0_self, w0_nb, w1_self, w1_nb, offs):
    idx = offs[:16].T.reshape(-1)
    x = f64(table).T
    msg = f64(w0_nb).T @ x[:, idx]
    h = np.maximum(f64(w0_self).T @ x + msg.reshape(M, K, S).sum(axis=1) / K, 0.0)
    return np.concatenate([f64(w1_self).T @ h, f64(w1_nb).T @ h], axis=0)

@@ -1,0 +1,100 @@
+import concourse.mybir as mybir
+from concourse.masks import make_identity
+
+BF16, F32, U16 = mybir.dt.bfloat16, mybir.dt.float32, mybir.dt.uint16
+
+P = 128
+S = 1024
+D = 128
+K = 4
+M = 256
+H = 2048
+HALF = 512
+NODE_BLOCKS = S // P
+NODE_HALVES = S // HALF
+M_BLOCKS = M // P
+H_BLOCKS = H // P
+OFFS_COLS = HALF // 16
+
+FLOPS = 2 * D * M * (S + K * S) + 2 * M * (2 * H) * S
+
+
+def tile_graphsage_b_kernel(tc, table, w0_self, w0_nb, w1_self, w1_nb, offs, out):
+    nc = tc.nc
+    with (
+        tc.tile_pool(name="held", bufs=1) as held,
+        tc.tile_pool(name="stage", bufs=8) as stage,
+    ):
+        rows = held.tile([P, NODE_BLOCKS, D], BF16, name="rows")
+        nc.sync.dma_start(rows[:], table.rearrange("(b p) d -> p b d", p=P))
+        offsets = held.tile([P, K * S // 16], U16, name="offsets")
+        nc.sync.dma_start(offsets[:], offs)
+        w0_self_sb = held.tile([D, M], BF16, name="w0_self_sb")
+        nc.scalar.dma_start(w0_self_sb[:], w0_self)
+        w0_nb_sb = held.tile([D, M], BF16, name="w0_nb_sb")
+        nc.scalar.dma_start(w0_nb_sb[:], w0_nb)
+        w1_sb = []
+        for name, w1 in (("w1_self_sb", w1_self), ("w1_nb_sb", w1_nb)):
+            w1_tile = held.tile([P, M_BLOCKS, H], BF16, name=name)
+            nc.gpsimd.dma_start(w1_tile[:], w1.rearrange("(kb p) q -> p kb q", p=P))
+            w1_sb.append(w1_tile)
+
+        w0_nb_quarter = held.tile([D, M], BF16, name="w0_nb_quarter")
+        nc.vector.tensor_scalar_mul(w0_nb_quarter[:], w0_nb_sb[:], 1.0 / K)
+
+        identity = held.tile([P, P], BF16, name="identity")
+        make_identity(nc, identity[:])
+        table_t = held.tile([D, S], BF16, name="table_t")
+        with tc.psum_pool(name="flip", bufs=2) as flip:
+            for nh in range(NODE_HALVES):
+                flipped = flip.tile([D, HALF], BF16, name="flipped")
+                for i in range(HALF // P):
+                    b = nh * (HALF // P) + i
+                    nc.tensor.transpose(flipped[:, i * P : (i + 1) * P], rows[:, b, :], identity[:])
+                nc.vector.tensor_copy(table_t[:, nh * HALF : (nh + 1) * HALF], flipped[:])
+
+        h = [held.tile([P, S], BF16, name=f"h{mb}") for mb in range(M_BLOCKS)]
+        with tc.psum_pool(name="sums", bufs=1) as sums:
+            groups = [(mb, nh) for mb in range(M_BLOCKS) for nh in range(NODE_HALVES)]
+            acc = {}
+            for mb, nh in groups:
+                acc[mb, nh] = sums.tile([P, HALF], F32, name=f"acc{mb}{nh}")
+                nc.tensor.matmul(
+                    acc[mb, nh][:],
+                    w0_self_sb[:, mb * P : (mb + 1) * P],
+                    table_t[:, nh * HALF : (nh + 1) * HALF],
+                    start=True,
+                    stop=False,
+                )
+            for mb, nh in groups:
+                for t in range(K):
+                    piece = t * NODE_HALVES + nh
+                    nc.tensor.matmul(
+                        acc[mb, nh][:],
+                        w0_nb_quarter[:, mb * P : (mb + 1) * P],
+                        table_t[:].indirect(offsets[:, piece * OFFS_COLS : (piece + 1) * OFFS_COLS]),
+                        start=False,
+                        stop=(t == K - 1),
+                    )
+                nc.vector.tensor_relu(h[mb][:, nh * HALF : (nh + 1) * HALF], acc[mb, nh][:])
+
+        with tc.psum_pool(name="prods", bufs=4) as prods:
+            for which in range(2):
+                for a in range(H_BLOCKS):
+                    staged = stage.tile([P, S], F32, name="staged")
+                    for nh in range(NODE_HALVES):
+                        prod = prods.tile([P, HALF], F32, name=f"prod{nh}")
+                        for kb in range(M_BLOCKS):
+                            nc.tensor.matmul(
+                                prod[:],
+                                w1_sb[which][:, kb, a * P : (a + 1) * P],
+                                h[kb][:, nh * HALF : (nh + 1) * HALF],
+                                start=(kb == 0),
+                                stop=(kb == M_BLOCKS - 1),
+                            )
+                        if nh == 0:
+                            nc.vector.tensor_copy(staged[:, :HALF], prod[:])
+                        else:
+                            nc.scalar.copy(staged[:, HALF:], prod[:])
+                    row = which * H + a * P
+                    nc.sync.dma_start(out[row : row + P, :], staged[:])

@@ -24,7 +24,11 @@ def tile_graphsage_b_kernel(tc, table, w0_self, w0_nb, w1_self, w1_nb, offs, out
     with (
         tc.tile_pool(name="held", bufs=1) as held,
         tc.tile_pool(name="stage", bufs=8) as stage,
+        tc.psum_pool(name="sums", bufs=1) as sums,
     ):
+        identity = held.tile([P, P], BF16, name="identity")
+        make_identity(nc, identity[:])
+
         rows = held.tile([P, NODE_BLOCKS, D], BF16, name="rows")
         nc.sync.dma_start(rows[:], table.rearrange("(b p) d -> p b d", p=P))
         offsets = held.tile([P, K * S // 16], U16, name="offsets")
@@ -36,14 +40,12 @@ def tile_graphsage_b_kernel(tc, table, w0_self, w0_nb, w1_self, w1_nb, offs, out
         w1_sb = []
         for name, w1 in (("w1_self_sb", w1_self), ("w1_nb_sb", w1_nb)):
             w1_tile = held.tile([P, M_BLOCKS, H], BF16, name=name)
-            nc.gpsimd.dma_start(w1_tile[:], w1.rearrange("(kb p) q -> p kb q", p=P))
+            nc.sync.dma_start(w1_tile[:], w1.rearrange("(kb p) q -> p kb q", p=P))
             w1_sb.append(w1_tile)
 
         w0_nb_quarter = held.tile([D, M], BF16, name="w0_nb_quarter")
         nc.vector.tensor_scalar_mul(w0_nb_quarter[:], w0_nb_sb[:], 1.0 / K)
 
-        identity = held.tile([P, P], BF16, name="identity")
-        make_identity(nc, identity[:])
         table_t = held.tile([D, S], BF16, name="table_t")
         with tc.psum_pool(name="flip", bufs=2) as flip:
             for nh in range(NODE_HALVES):
@@ -51,34 +53,36 @@ def tile_graphsage_b_kernel(tc, table, w0_self, w0_nb, w1_self, w1_nb, offs, out
                 for i in range(HALF // P):
                     b = nh * (HALF // P) + i
                     nc.tensor.transpose(flipped[:, i * P : (i + 1) * P], rows[:, b, :], identity[:])
-                nc.vector.tensor_copy(table_t[:, nh * HALF : (nh + 1) * HALF], flipped[:])
+                if nh == 0:
+                    nc.vector.tensor_copy(table_t[:, :HALF], flipped[:])
+                else:
+                    nc.scalar.copy(table_t[:, HALF:], flipped[:])
 
         h = [held.tile([P, S], BF16, name=f"h{mb}") for mb in range(M_BLOCKS)]
-        with tc.psum_pool(name="sums", bufs=1) as sums:
-            groups = [(mb, nh) for mb in range(M_BLOCKS) for nh in range(NODE_HALVES)]
-            acc = {}
-            for mb, nh in groups:
-                acc[mb, nh] = sums.tile([P, HALF], F32, name=f"acc{mb}{nh}")
+        groups = [(mb, nh) for nh in range(NODE_HALVES) for mb in range(M_BLOCKS)]
+        acc = {}
+        for mb, nh in groups:
+            acc[mb, nh] = sums.tile([P, HALF], F32, name=f"acc{mb}{nh}")
+            nc.tensor.matmul(
+                acc[mb, nh][:],
+                w0_self_sb[:, mb * P : (mb + 1) * P],
+                table_t[:, nh * HALF : (nh + 1) * HALF],
+                start=True,
+                stop=False,
+            )
+        for mb, nh in groups:
+            for t in range(K):
+                piece = t * NODE_HALVES + nh
                 nc.tensor.matmul(
                     acc[mb, nh][:],
-                    w0_self_sb[:, mb * P : (mb + 1) * P],
-                    table_t[:, nh * HALF : (nh + 1) * HALF],
-                    start=True,
-                    stop=False,
+                    w0_nb_quarter[:, mb * P : (mb + 1) * P],
+                    table_t[:].indirect(offsets[:, piece * OFFS_COLS : (piece + 1) * OFFS_COLS]),
+                    start=False,
+                    stop=(t == K - 1),
                 )
-            for mb, nh in groups:
-                for t in range(K):
-                    piece = t * NODE_HALVES + nh
-                    nc.tensor.matmul(
-                        acc[mb, nh][:],
-                        w0_nb_quarter[:, mb * P : (mb + 1) * P],
-                        table_t[:].indirect(offsets[:, piece * OFFS_COLS : (piece + 1) * OFFS_COLS]),
-                        start=False,
-                        stop=(t == K - 1),
-                    )
-                nc.vector.tensor_relu(h[mb][:, nh * HALF : (nh + 1) * HALF], acc[mb, nh][:])
+            nc.vector.tensor_relu(h[mb][:, nh * HALF : (nh + 1) * HALF], acc[mb, nh][:])
 
-        with tc.psum_pool(name="prods", bufs=4) as prods:
+        with tc.psum_pool(name="prods", bufs=2) as prods:
             for which in range(2):
                 for a in range(H_BLOCKS):
                     staged = stage.tile([P, S], F32, name="staged")

@@ -10,6 +10,7 @@ K = 4
 M = 256
 H = 2048
 HALF = 512
+PAIR = 2
 NODE_BLOCKS = S // P
 NODE_HALVES = S // HALF
 M_BLOCKS = M // P
@@ -30,18 +31,19 @@ def tile_graphsage_b_kernel(tc, table, w0_self, w0_nb, w1_self, w1_nb, offs, out
         make_identity(nc, identity[:])
 
         rows = held.tile([P, NODE_BLOCKS, D], BF16, name="rows")
-        nc.sync.dma_start(rows[:], table.rearrange("(b p) d -> p b d", p=P))
+        blocks = table.rearrange("(b p) d -> p b d", p=P)
+        for nh in range(NODE_HALVES):
+            half = slice(nh * (HALF // P), (nh + 1) * (HALF // P))
+            nc.sync.dma_start(rows[:, half, :], blocks[:, half, :])
         offsets = held.tile([P, K * S // 16], U16, name="offsets")
         nc.sync.dma_start(offsets[:], offs)
         w0_self_sb = held.tile([D, M], BF16, name="w0_self_sb")
         nc.scalar.dma_start(w0_self_sb[:], w0_self)
         w0_nb_sb = held.tile([D, M], BF16, name="w0_nb_sb")
         nc.scalar.dma_start(w0_nb_sb[:], w0_nb)
-        w1_sb = []
-        for name, w1 in (("w1_self_sb", w1_self), ("w1_nb_sb", w1_nb)):
-            w1_tile = held.tile([P, M_BLOCKS, H], BF16, name=name)
-            nc.sync.dma_start(w1_tile[:], w1.rearrange("(kb p) q -> p kb q", p=P))
-            w1_sb.append(w1_tile)
+        w1_sb = held.tile([P, M_BLOCKS, 2 * H], BF16, name="w1_sb")
+        for which, w1 in enumerate((w1_self, w1_nb)):
+            nc.sync.dma_start(w1_sb[:, :, which * H : (which + 1) * H], w1.rearrange("(kb p) q -> p kb q", p=P))
 
         w0_nb_quarter = held.tile([D, M], BF16, name="w0_nb_quarter")
         nc.vector.tensor_scalar_mul(w0_nb_quarter[:], w0_nb_sb[:], 1.0 / K)
@@ -59,46 +61,63 @@ def tile_graphsage_b_kernel(tc, table, w0_self, w0_nb, w1_self, w1_nb, offs, out
                     nc.scalar.copy(table_t[:, HALF:], flipped[:])
 
         h = [held.tile([P, S], BF16, name=f"h{mb}") for mb in range(M_BLOCKS)]
-        groups = [(mb, nh) for nh in range(NODE_HALVES) for mb in range(M_BLOCKS)]
-        acc = {}
-        for mb, nh in groups:
-            acc[mb, nh] = sums.tile([P, HALF], F32, name=f"acc{mb}{nh}")
-            nc.tensor.matmul(
-                acc[mb, nh][:],
-                w0_self_sb[:, mb * P : (mb + 1) * P],
-                table_t[:, nh * HALF : (nh + 1) * HALF],
-                start=True,
-                stop=False,
-            )
-        for mb, nh in groups:
-            for t in range(K):
-                piece = t * NODE_HALVES + nh
+        acc = {
+            (mb, nh): sums.tile([P, HALF], F32, name=f"acc{mb}{nh}")
+            for nh in range(NODE_HALVES)
+            for mb in range(M_BLOCKS)
+        }
+
+        def own_projections(nh):
+            for mb in range(M_BLOCKS):
                 nc.tensor.matmul(
                     acc[mb, nh][:],
-                    w0_nb_quarter[:, mb * P : (mb + 1) * P],
-                    table_t[:].indirect(offsets[:, piece * OFFS_COLS : (piece + 1) * OFFS_COLS]),
-                    start=False,
-                    stop=(t == K - 1),
+                    w0_self_sb[:, mb * P : (mb + 1) * P],
+                    table_t[:, nh * HALF : (nh + 1) * HALF],
+                    start=True,
+                    stop=False,
                 )
-            nc.vector.tensor_relu(h[mb][:, nh * HALF : (nh + 1) * HALF], acc[mb, nh][:])
 
+        def gathered_projections(nh):
+            for mb in range(M_BLOCKS):
+                for t in range(K):
+                    piece = t * NODE_HALVES + nh
+                    nc.tensor.matmul(
+                        acc[mb, nh][:],
+                        w0_nb_quarter[:, mb * P : (mb + 1) * P],
+                        table_t[:].indirect(offsets[:, piece * OFFS_COLS : (piece + 1) * OFFS_COLS]),
+                        start=False,
+                        stop=(t == K - 1),
+                    )
+                nc.vector.tensor_relu(h[mb][:, nh * HALF : (nh + 1) * HALF], acc[mb, nh][:])
+
+        def layer1(prods, nh, pairs):
+            nodes = slice(nh * HALF, (nh + 1) * HALF)
+            for pair in pairs:
+                staged = stage.tile([P, PAIR, HALF], F32, name="staged")
+                prod = [prods.tile([P, HALF], F32, name=f"prod{j}") for j in range(PAIR)]
+                for kb in range(M_BLOCKS):
+                    for j in range(PAIR):
+                        block = pair * PAIR + j
+                        nc.tensor.matmul(
+                            prod[j][:],
+                            w1_sb[:, kb, block * P : (block + 1) * P],
+                            h[kb][:, nodes],
+                            start=(kb == 0),
+                            stop=(kb == M_BLOCKS - 1),
+                        )
+                nc.vector.tensor_copy(staged[:, 0, :], prod[0][:])
+                nc.scalar.copy(staged[:, 1, :], prod[1][:])
+                row = pair * PAIR * P
+                nc.sync.dma_start(
+                    out[row : row + PAIR * P, nodes].rearrange("(j p) n -> p j n", p=P), staged[:]
+                )
+
+        pairs = list(range(2 * H_BLOCKS // PAIR))
         with tc.psum_pool(name="prods", bufs=2) as prods:
-            for which in range(2):
-                for a in range(H_BLOCKS):
-                    staged = stage.tile([P, S], F32, name="staged")
-                    for nh in range(NODE_HALVES):
-                        prod = prods.tile([P, HALF], F32, name=f"prod{nh}")
-                        for kb in range(M_BLOCKS):
-                            nc.tensor.matmul(
-                                prod[:],
-                                w1_sb[which][:, kb, a * P : (a + 1) * P],
-                                h[kb][:, nh * HALF : (nh + 1) * HALF],
-                                start=(kb == 0),
-                                stop=(kb == M_BLOCKS - 1),
-                            )
-                        if nh == 0:
-                            nc.vector.tensor_copy(staged[:, :HALF], prod[:])
-                        else:
-                            nc.scalar.copy(staged[:, HALF:], prod[:])
-                    row = which * H + a * P
-                    nc.sync.dma_start(out[row : row + P, :], staged[:])
+            own_projections(0)
+            gathered_projections(0)
+            own_projections(1)
+            layer1(prods, 0, pairs[:-1])
+            gathered_projections(1)
+            layer1(prods, 0, pairs[-1:])
+            layer1(prods, 1, pairs)

@@ -10,12 +10,13 @@ K = 4
 M = 256
 H = 2048
 HALF = 512
-PAIR = 2
 NODE_BLOCKS = S // P
 NODE_HALVES = S // HALF
 M_BLOCKS = M // P
-H_BLOCKS = H // P
 OFFS_COLS = HALF // 16
+
+ROWS_PER_PARTITION = [2] * 15 + [1] * 2
+assert P * sum(ROWS_PER_PARTITION) == 2 * H
 
 FLOPS = 2 * D * M * (S + K * S) + 2 * M * (2 * H) * S
 
@@ -24,7 +25,7 @@ def tile_graphsage_b_kernel(tc, table, w0_self, w0_nb, w1_self, w1_nb, offs, out
     nc = tc.nc
     with (
         tc.tile_pool(name="held", bufs=1) as held,
-        tc.tile_pool(name="stage", bufs=8) as stage,
+        tc.tile_pool(name="stage", bufs=4) as stage,
         tc.psum_pool(name="sums", bufs=1) as sums,
     ):
         identity = held.tile([P, P], BF16, name="identity")
@@ -67,57 +68,59 @@ def tile_graphsage_b_kernel(tc, table, w0_self, w0_nb, w1_self, w1_nb, offs, out
             for mb in range(M_BLOCKS)
         }
 
-        def own_projections(nh):
-            for mb in range(M_BLOCKS):
+        def own_projection(mb, nh, start, stop):
+            nc.tensor.matmul(
+                acc[mb, nh][:],
+                w0_self_sb[:, mb * P : (mb + 1) * P],
+                table_t[:, nh * HALF : (nh + 1) * HALF],
+                start=start,
+                stop=stop,
+            )
+
+        def gathered_projections(mb, nh, opens, closes):
+            for t in range(K):
+                piece = t * NODE_HALVES + nh
                 nc.tensor.matmul(
                     acc[mb, nh][:],
-                    w0_self_sb[:, mb * P : (mb + 1) * P],
-                    table_t[:, nh * HALF : (nh + 1) * HALF],
-                    start=True,
-                    stop=False,
+                    w0_nb_quarter[:, mb * P : (mb + 1) * P],
+                    table_t[:].indirect(offsets[:, piece * OFFS_COLS : (piece + 1) * OFFS_COLS]),
+                    start=(opens and t == 0),
+                    stop=(closes and t == K - 1),
                 )
 
-        def gathered_projections(nh):
-            for mb in range(M_BLOCKS):
-                for t in range(K):
-                    piece = t * NODE_HALVES + nh
-                    nc.tensor.matmul(
-                        acc[mb, nh][:],
-                        w0_nb_quarter[:, mb * P : (mb + 1) * P],
-                        table_t[:].indirect(offsets[:, piece * OFFS_COLS : (piece + 1) * OFFS_COLS]),
-                        start=False,
-                        stop=(t == K - 1),
-                    )
-                nc.vector.tensor_relu(h[mb][:, nh * HALF : (nh + 1) * HALF], acc[mb, nh][:])
+        for mb in range(M_BLOCKS):
+            own_projection(mb, 0, start=True, stop=False)
+        for mb in range(M_BLOCKS):
+            gathered_projections(mb, 0, opens=False, closes=True)
+            nc.vector.tensor_relu(h[mb][:, :HALF], acc[mb, 0][:])
+        for mb in range(M_BLOCKS):
+            gathered_projections(mb, 1, opens=True, closes=False)
+        for mb in range(M_BLOCKS):
+            own_projection(mb, 1, start=False, stop=True)
+        nc.vector.tensor_relu(h[0][:, HALF:], acc[0, 1][:])
+        nc.scalar.activation(h[1][:, HALF:], acc[1, 1][:], mybir.ActivationFunctionType.Relu)
 
-        def layer1(prods, nh, pairs):
-            nodes = slice(nh * HALF, (nh + 1) * HALF)
-            for pair in pairs:
-                staged = stage.tile([P, PAIR, HALF], F32, name="staged")
-                prod = [prods.tile([P, HALF], F32, name=f"prod{j}") for j in range(PAIR)]
-                for kb in range(M_BLOCKS):
-                    for j in range(PAIR):
-                        block = pair * PAIR + j
-                        nc.tensor.matmul(
-                            prod[j][:],
-                            w1_sb[:, kb, block * P : (block + 1) * P],
-                            h[kb][:, nodes],
-                            start=(kb == 0),
-                            stop=(kb == M_BLOCKS - 1),
-                        )
-                nc.vector.tensor_copy(staged[:, 0, :], prod[0][:])
-                nc.scalar.copy(staged[:, 1, :], prod[1][:])
-                row = pair * PAIR * P
+        with tc.psum_pool(name="prods", bufs=4) as prods:
+            first_row = 0
+            for r in ROWS_PER_PARTITION:
+                staged = stage.tile([P, r, S], F32, name=f"staged{r}")
+                for nh in range(NODE_HALVES):
+                    nodes = slice(nh * HALF, (nh + 1) * HALF)
+                    for j in range(r):
+                        prod = prods.tile([P, HALF], F32, name="prod")
+                        for kb in range(M_BLOCKS):
+                            nc.tensor.matmul(
+                                prod[:],
+                                w1_sb[:, kb, first_row + j : first_row + r * P : r],
+                                h[kb][:, nodes],
+                                start=(kb == 0),
+                                stop=(kb == M_BLOCKS - 1),
+                            )
+                        if (nh * r + j) % 2 == 0:
+                            nc.vector.tensor_copy(staged[:, j, nodes], prod[:])
+                        else:
+                            nc.scalar.copy(staged[:, j, nodes], prod[:])
                 nc.sync.dma_start(
-                    out[row : row + PAIR * P, nodes].rearrange("(j p) n -> p j n", p=P), staged[:]
+                    out[first_row : first_row + r * P, :].rearrange("(p j) n -> p j n", j=r), staged[:]
                 )
-
-        pairs = list(range(2 * H_BLOCKS // PAIR))
-        with tc.psum_pool(name="prods", bufs=2) as prods:
-            own_projections(0)
-            gathered_projections(0)
-            own_projections(1)
-            layer1(prods, 0, pairs[:-1])
-            gathered_projections(1)
-            layer1(prods, 0, pairs[-1:])
-            layer1(prods, 1, pairs)
+                first_row += r * P

@@ -15,7 +15,7 @@ NODE_HALVES = S // HALF
 M_BLOCKS = M // P
 OFFS_COLS = HALF // 16
 
-ROWS_PER_PARTITION = [2] * 15 + [1] * 2
+ROWS_PER_PARTITION = [1] * 16 + [2] * 7 + [1] * 2
 assert P * sum(ROWS_PER_PARTITION) == 2 * H
 
 FLOPS = 2 * D * M * (S + K * S) + 2 * M * (2 * H) * S
@@ -25,7 +25,7 @@ def tile_graphsage_b_kernel(tc, table, w0_self, w0_nb, w1_self, w1_nb, offs, out
     nc = tc.nc
     with (
         tc.tile_pool(name="held", bufs=1) as held,
-        tc.tile_pool(name="stage", bufs=4) as stage,
+        tc.tile_pool(name="stage", bufs=6) as stage,
         tc.psum_pool(name="sums", bufs=1) as sums,
     ):
         identity = held.tile([P, P], BF16, name="identity")

import concourse.mybir as mybir
from concourse.masks import make_identity

BF16, F32, U16 = mybir.dt.bfloat16, mybir.dt.float32, mybir.dt.uint16

P = 128
S = 1024
D = 128
K = 4
M = 256
H = 2048
HALF = 512
NODE_BLOCKS = S // P
NODE_HALVES = S // HALF
M_BLOCKS = M // P
OFFS_COLS = HALF // 16

ROWS_PER_PARTITION = [1] * 16 + [2] * 7 + [1] * 2
assert P * sum(ROWS_PER_PARTITION) == 2 * H

FLOPS = 2 * D * M * (S + K * S) + 2 * M * (2 * H) * S


def tile_graphsage_b_kernel(tc, table, w0_self, w0_nb, w1_self, w1_nb, offs, out):
    nc = tc.nc
    with (
        tc.tile_pool(name="held", bufs=1) as held,
        tc.tile_pool(name="stage", bufs=6) as stage,
        tc.psum_pool(name="sums", bufs=1) as sums,
    ):
        identity = held.tile([P, P], BF16, name="identity")
        make_identity(nc, identity[:])

        rows = held.tile([P, NODE_BLOCKS, D], BF16, name="rows")
        blocks = table.rearrange("(b p) d -> p b d", p=P)
        for nh in range(NODE_HALVES):
            half = slice(nh * (HALF // P), (nh + 1) * (HALF // P))
            nc.sync.dma_start(rows[:, half, :], blocks[:, half, :])
        offsets = held.tile([P, K * S // 16], U16, name="offsets")
        nc.sync.dma_start(offsets[:], offs)
        w0_self_sb = held.tile([D, M], BF16, name="w0_self_sb")
        nc.scalar.dma_start(w0_self_sb[:], w0_self)
        w0_nb_sb = held.tile([D, M], BF16, name="w0_nb_sb")
        nc.scalar.dma_start(w0_nb_sb[:], w0_nb)
        w1_sb = held.tile([P, M_BLOCKS, 2 * H], BF16, name="w1_sb")
        for which, w1 in enumerate((w1_self, w1_nb)):
            nc.sync.dma_start(w1_sb[:, :, which * H : (which + 1) * H], w1.rearrange("(kb p) q -> p kb q", p=P))

        w0_nb_quarter = held.tile([D, M], BF16, name="w0_nb_quarter")
        nc.vector.tensor_scalar_mul(w0_nb_quarter[:], w0_nb_sb[:], 1.0 / K)

        table_t = held.tile([D, S], BF16, name="table_t")
        with tc.psum_pool(name="flip", bufs=2) as flip:
            for nh in range(NODE_HALVES):
                flipped = flip.tile([D, HALF], BF16, name="flipped")
                for i in range(HALF // P):
                    b = nh * (HALF // P) + i
                    nc.tensor.transpose(flipped[:, i * P : (i + 1) * P], rows[:, b, :], identity[:])
                if nh == 0:
                    nc.vector.tensor_copy(table_t[:, :HALF], flipped[:])
                else:
                    nc.scalar.copy(table_t[:, HALF:], flipped[:])

        h = [held.tile([P, S], BF16, name=f"h{mb}") for mb in range(M_BLOCKS)]
        acc = {
            (mb, nh): sums.tile([P, HALF], F32, name=f"acc{mb}{nh}")
            for nh in range(NODE_HALVES)
            for mb in range(M_BLOCKS)
        }

        def own_projection(mb, nh, start, stop):
            nc.tensor.matmul(
                acc[mb, nh][:],
                w0_self_sb[:, mb * P : (mb + 1) * P],
                table_t[:, nh * HALF : (nh + 1) * HALF],
                start=start,
                stop=stop,
            )

        def gathered_projections(mb, nh, opens, closes):
            for t in range(K):
                piece = t * NODE_HALVES + nh
                nc.tensor.matmul(
                    acc[mb, nh][:],
                    w0_nb_quarter[:, mb * P : (mb + 1) * P],
                    table_t[:].indirect(offsets[:, piece * OFFS_COLS : (piece + 1) * OFFS_COLS]),
                    start=(opens and t == 0),
                    stop=(closes and t == K - 1),
                )

        for mb in range(M_BLOCKS):
            own_projection(mb, 0, start=True, stop=False)
        for mb in range(M_BLOCKS):
            gathered_projections(mb, 0, opens=False, closes=True)
            nc.vector.tensor_relu(h[mb][:, :HALF], acc[mb, 0][:])
        for mb in range(M_BLOCKS):
            gathered_projections(mb, 1, opens=True, closes=False)
        for mb in range(M_BLOCKS):
            own_projection(mb, 1, start=False, stop=True)
        nc.vector.tensor_relu(h[0][:, HALF:], acc[0, 1][:])
        nc.scalar.activation(h[1][:, HALF:], acc[1, 1][:], mybir.ActivationFunctionType.Relu)

        with tc.psum_pool(name="prods", bufs=4) as prods:
            first_row = 0
            for r in ROWS_PER_PARTITION:
                staged = stage.tile([P, r, S], F32, name=f"staged{r}")
                for nh in range(NODE_HALVES):
                    nodes = slice(nh * HALF, (nh + 1) * HALF)
                    for j in range(r):
                        prod = prods.tile([P, HALF], F32, name="prod")
                        for kb in range(M_BLOCKS):
                            nc.tensor.matmul(
                                prod[:],
                                w1_sb[:, kb, first_row + j : first_row + r * P : r],
                                h[kb][:, nodes],
                                start=(kb == 0),
                                stop=(kb == M_BLOCKS - 1),
                            )
                        if (nh * r + j) % 2 == 0:
                            nc.vector.tensor_copy(staged[:, j, nodes], prod[:])
                        else:
                            nc.scalar.copy(staged[:, j, nodes], prod[:])
                nc.sync.dma_start(
                    out[first_row : first_row + r * P, :].rearrange("(p j) n -> p j n", j=r), staged[:]
                )
                first_row += r * P
